import numpy as np
import ml_dtypes


def mxq(x, axis, fmt="e4m3"):
    dtype, down = {"e4m3": (ml_dtypes.float8_e4m3fn, 7), "e5m2": (ml_dtypes.float8_e5m2, 14)}[fmt]
    v = np.moveaxis(np.asarray(x, np.float32).astype(ml_dtypes.bfloat16).astype(np.float64), axis, -1)
    blocks = v.reshape(v.shape[:-1] + (-1, 32))
    amax = np.abs(blocks).max(-1, keepdims=True)
    byte = np.maximum(np.where(amax > 0, np.frexp(amax)[1] - 1 + 127, 0) - down, 1)
    scale = np.exp2(byte - 127.0)
    codes = (blocks / scale).astype(np.float32).astype(dtype).astype(np.float64)
    return np.moveaxis((codes * scale).reshape(v.shape), -1, axis)


WIDE = False


def mx_kscale(k):
    if not WIDE:
        return np.ones(k)
    levels = np.array([10, -10, 5, -5, 0])
    a = np.random.permutation(np.resize(levels, k // 512 * 4)).reshape(k // 512, 4)
    idx = np.arange(k)
    return np.exp2(a[idx // 512, idx % 128 // 32])


BF16 = ml_dtypes.bfloat16


def bf(x):
    return np.asarray(x, np.float32).astype(BF16)


def f64(x):
    return np.asarray(x).astype(np.float64)


E2M1 = np.array([0.0, 0.5, 1.0, 1.5, 2.0, 3.0, 4.0, 6.0, -0.0, -0.5, -1.0, -1.5, -2.0, -3.0, -4.0, -6.0])


def pack_weight(w, fmt):
    k, n = w.shape
    w = f64(bf(w)).reshape(k // 32, 32, n)
    amax = np.abs(w).max(1)
    if fmt == "e4m3":
        byte = np.frexp(amax)[1] - 1 + 127 - 7
    else:
        mant, ex = np.frexp(amax / 6.0)
        byte = np.where(mant > 0.5, ex, ex - 1) + 127
    byte = np.clip(np.where(amax > 0, byte, 1), 1, 254)
    scaled = (w * np.exp2(127.0 - byte)[:, None, :]).reshape(k, n).astype(np.float32)
    by_word = np.ascontiguousarray(scaled.reshape(k // 512, 128, 4, n).transpose(0, 1, 3, 2))
    if fmt == "e4m3":
        words = by_word.astype(ml_dtypes.float8_e4m3fn).view(np.uint8)
    else:
        c = by_word.astype(ml_dtypes.float4_e2m1fn).view(np.uint8) & 0xF
        words = c[..., 0::2] | (c[..., 1::2] << 4)
    return np.ascontiguousarray(words), np.ascontiguousarray(byte.astype(np.uint8).reshape(k // 512, 16, n))


def unpack_weight(words, scales, fmt):
    g, p, n, _ = words.shape
    if fmt == "e4m3":
        vals = np.ascontiguousarray(words).view(ml_dtypes.float8_e4m3fn).astype(np.float64)
    else:
        nib = np.empty((g, p, n, 4), np.uint8)
        nib[..., 0::2] = words & 0xF
        nib[..., 1::2] = words >> 4
        vals = E2M1[nib]
    vals = vals * np.repeat(np.exp2(scales.astype(np.float64) - 127.0), 8, axis=1)[..., None]
    return vals.transpose(0, 1, 3, 2).reshape(g * 512, n)


B, S, H, I = 2, 64, 8192, 1024
FMT = "e4m3"


def silu(v):
    return v / (1.0 + np.exp(-v))


def ternary(shape):
    return np.random.randint(-1, 2, shape).astype(np.float64)


def setup_inputs():
    s, t = mx_kscale(H), mx_kscale(I)
    x = np.random.standard_normal((B, S, H)) * s
    gate_w = ternary((I, H)) / s[None, :]
    up_w = ternary((I, H)) / s[None, :]
    down_w = ternary((H, I)) / t[None, :]
    gate_s = np.random.uniform(0.5, 2.5, I) / np.sqrt(H)
    up_s = np.random.uniform(0.5, 2.5, I) / np.sqrt(H) * t
    down_s = np.random.uniform(0.5, 2.5, H) / np.sqrt(I)
    gate_w_words, gate_w_scales = pack_weight(np.ascontiguousarray(gate_w.T), FMT)
    up_w_words, up_w_scales = pack_weight(np.ascontiguousarray(up_w.T), FMT)
    down_w_words, down_w_scales = pack_weight(np.ascontiguousarray(down_w.T), FMT)
    return {"x": bf(x), "gate_w_words": gate_w_words, "gate_w_scales": gate_w_scales,
            "up_w_words": up_w_words, "up_w_scales": up_w_scales,
            "down_w_words": down_w_words, "down_w_scales": down_w_scales,
            "gate_s": bf(gate_s), "up_s": bf(up_s), "down_s": bf(down_s)}


def reference(x, gate_w_words, gate_w_scales, up_w_words, up_w_scales, down_w_words, down_w_scales, gate_s, up_s, down_s):
    x = f64(x)
    b, s, h = x.shape
    xq = mxq(x.reshape(b * s, h), 1, "e4m3")
    g = (xq @ unpack_weight(gate_w_words, gate_w_scales, FMT)) * f64(gate_s)
    u = (xq @ unpack_weight(up_w_words, up_w_scales, FMT)) * f64(up_s)
    hdn = silu(g) * u
    out = (mxq(hdn, 1, "e4m3") @ unpack_weight(down_w_words, down_w_scales, FMT)) * f64(down_s)
    return out.reshape(b, s, -1)

@@ -1,0 +1,223 @@
+from contextlib import ExitStack
+
+import concourse.mybir as mybir
+from concourse.masks import make_identity
+
+F32 = mybir.dt.float32
+BF16 = mybir.dt.bfloat16
+I32 = mybir.dt.int32
+U32 = mybir.dt.uint32
+U8 = mybir.dt.uint8
+FP8X4 = mybir.dt.float8_e4m3fn_x4
+MULT = mybir.AluOpType.mult
+SILU = mybir.ActivationFunctionType.Silu
+
+P = 128
+HIDDEN = 8192
+INNER = 1024
+K_PASS = 512
+N_TILE = 512
+PASSES_1 = HIDDEN // K_PASS
+PASSES_2 = INNER // K_PASS
+CHUNK_COLS = 1024
+CHUNKS_1 = PASSES_1 // 2
+CHUNKS_2 = HIDDEN // CHUNK_COLS
+RING = 12
+SHARED = 4
+GATE_ROW = 0
+UP_ROW = GATE_ROW + INNER // N_TILE
+DOWN_ROW = UP_ROW + INNER // N_TILE
+S_ROWS = DOWN_ROW + HIDDEN // N_TILE
+
+FLOPS = 2 * P * HIDDEN * INNER * 3
+
+
+def load_shared_planes(nc, planes, scale_rows):
+    for quadrant in range(4):
+        nc.sync.dma_start(
+            out=planes[32 * quadrant : 32 * quadrant + 4 * SHARED, :].bitcast(I32),
+            in_=scale_rows[:, 4 * quadrant : 4 * quadrant + 4, :].bitcast(I32),
+        )
+
+
+def tile_cudaternaryexpertmodule_k_kernel(
+    tc,
+    x,
+    gate_w_words,
+    gate_w_scales,
+    up_w_words,
+    up_w_scales,
+    down_w_words,
+    down_w_scales,
+    gate_s,
+    up_s,
+    down_s,
+    out,
+):
+    nc = tc.nc
+    x_rows = x.flatten_outer_dims()
+    out_rows = out.flatten_outer_dims()
+    gate_src = gate_w_words.rearrange("g p n t -> p g (n t)").bitcast(I32)
+    up_src = up_w_words.rearrange("g p n t -> p g (n t)").bitcast(I32)
+    down_src = down_w_words.rearrange("g p n t -> p g (n t)").bitcast(I32)
+
+    with ExitStack() as ctx:
+        keep = ctx.enter_context(tc.tile_pool(name="keep", bufs=1))
+        ring = ctx.enter_context(tc.tile_pool(name="ring", bufs=RING))
+        work = ctx.enter_context(tc.tile_pool(name="work", bufs=3))
+        results = ctx.enter_context(tc.tile_pool(name="results", bufs=CHUNKS_2))
+        psum_acc = ctx.enter_context(tc.psum_pool(name="psum_acc", bufs=4))
+        psum_aux = ctx.enter_context(tc.psum_pool(name="psum_aux", bufs=4))
+
+        x_sb = keep.tile([P, HIDDEN], BF16)
+        for quarter in range(4):
+            cols = slice(quarter * 2048, (quarter + 1) * 2048)
+            nc.sync.dma_start(out=x_sb[:, cols], in_=x_rows[:, cols])
+
+        gate_planes = keep.tile([P, PASSES_1 // SHARED, INNER], U8, align_bytes=64)
+        up_planes = keep.tile([P, PASSES_1 // SHARED, INNER], U8, align_bytes=64)
+        down_planes = keep.tile([P, PASSES_2, HIDDEN // SHARED], U8, align_bytes=64)
+        for planes in (gate_planes, up_planes, down_planes):
+            nc.vector.memset(planes[:].bitcast(I32), 0)
+
+        for block in range(PASSES_1 // SHARED):
+            for planes, scales in ((gate_planes, gate_w_scales), (up_planes, up_w_scales)):
+                load_shared_planes(
+                    nc, planes[:, block, :], scales[SHARED * block : SHARED * (block + 1), :, :]
+                )
+
+        ident_f32 = keep.tile([P, P], F32)
+        make_identity(nc, ident_f32[:])
+        ident_bf16 = keep.tile([P, P], BF16)
+        make_identity(nc, ident_bf16[:])
+        s_rows = keep.tile([P, N_TILE], BF16)
+        nc.vector.memset(s_rows[:], 0.0)
+        nc.scalar.dma_start(out=s_rows[GATE_ROW:UP_ROW, :], in_=gate_s.rearrange("(r c) -> r c", c=N_TILE))
+        nc.scalar.dma_start(out=s_rows[UP_ROW:DOWN_ROW, :], in_=up_s.rearrange("(r c) -> r c", c=N_TILE))
+        nc.scalar.dma_start(out=s_rows[DOWN_ROW:S_ROWS, :], in_=down_s.rearrange("(r c) -> r c", c=N_TILE))
+
+        x_codes = keep.tile([P, PASSES_1 * P], U32, align_bytes=64)
+        x_scales = keep.tile([P, PASSES_1 * P], U8, align_bytes=64)
+        x_words = x_sb[:].bitcast(F32)
+        for pair in range(PASSES_1 // 2):
+            xt = psum_aux.tile([P, 2, 2, P], F32, tag="aux")
+            for i in range(2):
+                g = 2 * pair + i
+                for u in range(2):
+                    nc.tensor.transpose(
+                        xt[:, i, u, :], x_words[:, 256 * g + u : 256 * (g + 1) : 2], ident_f32[:]
+                    )
+            x_grouped = work.tile([P, 2 * K_PASS], BF16, align_bytes=64)
+            grouped_words = x_grouped[:].bitcast(F32).rearrange("p (i r u) -> p i r u", i=2, u=2)
+            if pair % 2 == 0:
+                nc.vector.tensor_copy(out=grouped_words, in_=xt[:].rearrange("p i u r -> p i r u"))
+            else:
+                nc.scalar.copy(out=grouped_words, in_=xt[:].rearrange("p i u r -> p i r u"))
+            cols = slice(2 * P * pair, 2 * P * (pair + 1))
+            nc.vector.quantize_mx(
+                out=x_codes[:, cols].bitcast(FP8X4), scales=x_scales[:, cols], in_=x_grouped[:]
+            )
+
+        s_bcast = keep.tile([P, S_ROWS, N_TILE], BF16)
+        for r in range(S_ROWS):
+            spread = psum_aux.tile([P, N_TILE], F32, tag="aux")
+            nc.tensor.matmul(
+                out=spread[:],
+                lhsT=ident_bf16[:, r : r + 1].to_broadcast([P, P]),
+                rhs=s_rows[:],
+                start=True,
+                stop=True,
+            )
+            nc.scalar.copy(out=s_bcast[:, r, :], in_=spread[:])
+
+        acc_gate = [psum_acc.tile([P, N_TILE], F32, tag="acc", name="acc_gate%d" % h) for h in range(2)]
+        acc_up = [psum_acc.tile([P, N_TILE], F32, tag="acc", name="acc_up%d" % h) for h in range(2)]
+        for chunk in range(CHUNKS_1):
+            gate_words = ring.tile([P, 2, CHUNK_COLS], U32, tag="words", align_bytes=64)
+            nc.sync.dma_start(out=gate_words[:].bitcast(I32), in_=gate_src[:, 2 * chunk : 2 * chunk + 2, :])
+            up_words = ring.tile([P, 2, CHUNK_COLS], U32, tag="words", align_bytes=64)
+            nc.sync.dma_start(out=up_words[:].bitcast(I32), in_=up_src[:, 2 * chunk : 2 * chunk + 2, :])
+            for i in range(2):
+                g = 2 * chunk + i
+                tokens = slice(P * g, P * (g + 1))
+                for h in range(2):
+                    cols = slice(N_TILE * h, N_TILE * (h + 1))
+                    for acc, words, planes in (
+                        (acc_gate[h], gate_words, gate_planes),
+                        (acc_up[h], up_words, up_planes),
+                    ):
+                        nc.tensor.matmul_mx(
+                            out=acc[:],
+                            lhsT=x_codes[:, tokens].bitcast(FP8X4),
+                            lhsT_scale=x_scales[:, tokens],
+                            rhs=words[:, i, cols].bitcast(FP8X4),
+                            rhs_scale=planes[4 * (g % SHARED) : P, g // SHARED, cols],
+                            start=(g == 0),
+                            stop=(g == PASSES_1 - 1),
+                        )
+
+        for g in range(PASSES_2):
+            load_shared_planes(
+                nc, down_planes[:, g, :], down_w_scales[g].rearrange("q (j n) -> j q n", j=SHARED)
+            )
+        down_words = []
+        for chunk in range(CHUNKS_2):
+            words = ring.tile([P, PASSES_2, CHUNK_COLS], U32, tag="words", align_bytes=64, name="down_words%d" % chunk)
+            nc.sync.dma_start(
+                out=words[:].bitcast(I32),
+                in_=down_src[:, :, CHUNK_COLS * chunk : CHUNK_COLS * (chunk + 1)],
+            )
+            down_words.append(words)
+
+        hdn = keep.tile([P, INNER], BF16)
+        h_codes = keep.tile([P, PASSES_2 * P], U32, align_bytes=64)
+        h_scales = keep.tile([P, PASSES_2 * P], U8, align_bytes=64)
+        for g in range(PASSES_2):
+            gate_f = work.tile([P, N_TILE], F32)
+            nc.vector.tensor_tensor(out=gate_f[:], in0=acc_gate[g][:], in1=s_bcast[:, GATE_ROW + g, :], op=MULT)
+            silu_f = work.tile([P, N_TILE], F32)
+            nc.scalar.activation(out=silu_f[:], in_=gate_f[:], func=SILU)
+            up_f = work.tile([P, N_TILE], F32)
+            nc.vector.tensor_tensor(out=up_f[:], in0=acc_up[g][:], in1=s_bcast[:, UP_ROW + g, :], op=MULT)
+            nc.vector.tensor_tensor(
+                out=hdn[:, K_PASS * g : K_PASS * (g + 1)], in0=silu_f[:], in1=up_f[:], op=MULT
+            )
+            ht = psum_aux.tile([P, 4, P], BF16, tag="aux")
+            for t in range(4):
+                nc.tensor.transpose(
+                    ht[:, t, :], hdn[:, K_PASS * g + t : K_PASS * (g + 1) : 4], ident_bf16[:]
+                )
+            h_grouped = work.tile([P, P, 4], BF16, align_bytes=64)
+            nc.scalar.copy(out=h_grouped[:], in_=ht[:].rearrange("p t r -> p r t"))
+            tokens = slice(P * g, P * (g + 1))
+            nc.vector.quantize_mx(
+                out=h_codes[:, tokens].bitcast(FP8X4),
+                scales=h_scales[:, tokens],
+                in_=h_grouped[:].rearrange("p r t -> p (r t)"),
+            )
+
+        for chunk in range(CHUNKS_2):
+            result = results.tile([P, CHUNK_COLS], F32)
+            for h in range(CHUNK_COLS // N_TILE):
+                first = CHUNK_COLS * chunk + N_TILE * h
+                j, n = divmod(first, HIDDEN // SHARED)
+                acc_out = psum_acc.tile([P, N_TILE], F32, tag="acc")
+                for g in range(PASSES_2):
+                    nc.tensor.matmul_mx(
+                        out=acc_out[:],
+                        lhsT=h_codes[:, P * g : P * (g + 1)].bitcast(FP8X4),
+                        lhsT_scale=h_scales[:, P * g : P * (g + 1)],
+                        rhs=down_words[chunk][:, g, N_TILE * h : N_TILE * (h + 1)].bitcast(FP8X4),
+                        rhs_scale=down_planes[4 * j : P, g, n : n + N_TILE],
+                        start=(g == 0),
+                        stop=(g == PASSES_2 - 1),
+                    )
+                nc.vector.tensor_tensor(
+                    out=result[:, N_TILE * h : N_TILE * (h + 1)],
+                    in0=acc_out[:],
+                    in1=s_bcast[:, DOWN_ROW + first // N_TILE, :],
+                    op=MULT,
+                )
+            nc.sync.dma_start(
+                out=out_rows[:, CHUNK_COLS * chunk : CHUNK_COLS * (chunk + 1)], in_=result[:]
+            )

@@ -34,9 +34,9 @@ FLOPS = 2 * P * HIDDEN * INNER * 3
 
 def load_shared_planes(nc, planes, scale_rows):
     for quadrant in range(4):
-        nc.sync.dma_start(
-            out=planes[32 * quadrant : 32 * quadrant + 4 * SHARED, :].bitcast(I32),
-            in_=scale_rows[:, 4 * quadrant : 4 * quadrant + 4, :].bitcast(I32),
+        nc.gpsimd.dma_start(
+            out=planes[32 * quadrant : 32 * quadrant + 4 * SHARED, :].bitcast(F32),
+            in_=scale_rows[:, 4 * quadrant : 4 * quadrant + 4, :].bitcast(F32),
         )
 
 
@@ -74,6 +74,11 @@ def tile_cudaternaryexpertmodule_k_kernel(
             cols = slice(quarter * 2048, (quarter + 1) * 2048)
             nc.sync.dma_start(out=x_sb[:, cols], in_=x_rows[:, cols])
 
+        ident_f32 = keep.tile([P, P], F32)
+        make_identity(nc, ident_f32[:])
+        ident_bf16 = keep.tile([P, P], BF16)
+        make_identity(nc, ident_bf16[:])
+
         gate_planes = keep.tile([P, PASSES_1 // SHARED, INNER], U8, align_bytes=64)
         up_planes = keep.tile([P, PASSES_1 // SHARED, INNER], U8, align_bytes=64)
         down_planes = keep.tile([P, PASSES_2, HIDDEN // SHARED], U8, align_bytes=64)
@@ -85,11 +90,11 @@ def tile_cudaternaryexpertmodule_k_kernel(
                 load_shared_planes(
                     nc, planes[:, block, :], scales[SHARED * block : SHARED * (block + 1), :, :]
                 )
+        for g in range(PASSES_2):
+            load_shared_planes(
+                nc, down_planes[:, g, :], down_w_scales[g].rearrange("q (j n) -> j q n", j=SHARED)
+            )
 
-        ident_f32 = keep.tile([P, P], F32)
-        make_identity(nc, ident_f32[:])
-        ident_bf16 = keep.tile([P, P], BF16)
-        make_identity(nc, ident_bf16[:])
         s_rows = keep.tile([P, N_TILE], BF16)
         nc.vector.memset(s_rows[:], 0.0)
         nc.scalar.dma_start(out=s_rows[GATE_ROW:UP_ROW, :], in_=gate_s.rearrange("(r c) -> r c", c=N_TILE))
@@ -156,10 +161,6 @@ def tile_cudaternaryexpertmodule_k_kernel(
                             stop=(g == PASSES_1 - 1),
                         )
 
-        for g in range(PASSES_2):
-            load_shared_planes(
-                nc, down_planes[:, g, :], down_w_scales[g].rearrange("q (j n) -> j q n", j=SHARED)
-            )
         down_words = []
         for chunk in range(CHUNKS_2):
             words = ring.tile([P, PASSES_2, CHUNK_COLS], U32, tag="words", align_bytes=64, name="down_words%d" % chunk)

@@ -19,11 +19,11 @@ K_PASS = 512
 N_TILE = 512
 PASSES_1 = HIDDEN // K_PASS
 PASSES_2 = INNER // K_PASS
-CHUNK_COLS = 1024
-CHUNKS_1 = PASSES_1 // 2
-CHUNKS_2 = HIDDEN // CHUNK_COLS
-RING = 12
 SHARED = 4
+CHUNKS_1 = PASSES_1 // SHARED
+CHUNKS_2 = SHARED
+DOWN_COLS = HIDDEN // CHUNKS_2
+RING = 6
 GATE_ROW = 0
 UP_ROW = GATE_ROW + INNER // N_TILE
 DOWN_ROW = UP_ROW + INNER // N_TILE
@@ -70,8 +70,8 @@ def tile_cudaternaryexpertmodule_k_kernel(
         psum_aux = ctx.enter_context(tc.psum_pool(name="psum_aux", bufs=4))
 
         x_sb = keep.tile([P, HIDDEN], BF16)
-        for quarter in range(4):
-            cols = slice(quarter * 2048, (quarter + 1) * 2048)
+        for half in range(2):
+            cols = slice(half * HIDDEN // 2, (half + 1) * HIDDEN // 2)
             nc.sync.dma_start(out=x_sb[:, cols], in_=x_rows[:, cols])
 
         ident_f32 = keep.tile([P, P], F32)
@@ -79,16 +79,16 @@ def tile_cudaternaryexpertmodule_k_kernel(
         ident_bf16 = keep.tile([P, P], BF16)
         make_identity(nc, ident_bf16[:])
 
-        gate_planes = keep.tile([P, PASSES_1 // SHARED, INNER], U8, align_bytes=64)
-        up_planes = keep.tile([P, PASSES_1 // SHARED, INNER], U8, align_bytes=64)
-        down_planes = keep.tile([P, PASSES_2, HIDDEN // SHARED], U8, align_bytes=64)
+        gate_planes = keep.tile([P, CHUNKS_1, INNER], U8, align_bytes=64)
+        up_planes = keep.tile([P, CHUNKS_1, INNER], U8, align_bytes=64)
+        down_planes = keep.tile([P, PASSES_2, DOWN_COLS], U8, align_bytes=64)
         for planes in (gate_planes, up_planes, down_planes):
             nc.vector.memset(planes[:].bitcast(I32), 0)
 
-        for block in range(PASSES_1 // SHARED):
+        for chunk in range(CHUNKS_1):
             for planes, scales in ((gate_planes, gate_w_scales), (up_planes, up_w_scales)):
                 load_shared_planes(
-                    nc, planes[:, block, :], scales[SHARED * block : SHARED * (block + 1), :, :]
+                    nc, planes[:, chunk, :], scales[SHARED * chunk : SHARED * (chunk + 1), :, :]
                 )
         for g in range(PASSES_2):
             load_shared_planes(
@@ -138,35 +138,38 @@ def tile_cudaternaryexpertmodule_k_kernel(
         acc_gate = [psum_acc.tile([P, N_TILE], F32, tag="acc", name="acc_gate%d" % h) for h in range(2)]
         acc_up = [psum_acc.tile([P, N_TILE], F32, tag="acc", name="acc_up%d" % h) for h in range(2)]
         for chunk in range(CHUNKS_1):
-            gate_words = ring.tile([P, 2, CHUNK_COLS], U32, tag="words", align_bytes=64)
-            nc.sync.dma_start(out=gate_words[:].bitcast(I32), in_=gate_src[:, 2 * chunk : 2 * chunk + 2, :])
-            up_words = ring.tile([P, 2, CHUNK_COLS], U32, tag="words", align_bytes=64)
-            nc.sync.dma_start(out=up_words[:].bitcast(I32), in_=up_src[:, 2 * chunk : 2 * chunk + 2, :])
-            for i in range(2):
-                g = 2 * chunk + i
-                tokens = slice(P * g, P * (g + 1))
-                for h in range(2):
-                    cols = slice(N_TILE * h, N_TILE * (h + 1))
-                    for acc, words, planes in (
-                        (acc_gate[h], gate_words, gate_planes),
-                        (acc_up[h], up_words, up_planes),
-                    ):
+            passes = slice(SHARED * chunk, SHARED * (chunk + 1))
+            gate_words = ring.tile([P, SHARED, INNER], U32, tag="words", align_bytes=64)
+            nc.sync.dma_start(out=gate_words[:].bitcast(I32), in_=gate_src[:, passes, :])
+            up_words = ring.tile([P, SHARED, INNER], U32, tag="words", align_bytes=64)
+            nc.sync.dma_start(out=up_words[:].bitcast(I32), in_=up_src[:, passes, :])
+            for acc, words, planes in (
+                (acc_gate, gate_words, gate_planes),
+                (acc_up, up_words, up_planes),
+            ):
+                for j in range(SHARED):
+                    g = SHARED * chunk + j
+                    tokens = slice(P * g, P * (g + 1))
+                    for h in range(INNER // N_TILE):
+                        cols = slice(N_TILE * h, N_TILE * (h + 1))
                         nc.tensor.matmul_mx(
-                            out=acc[:],
+                            out=acc[h][:],
                             lhsT=x_codes[:, tokens].bitcast(FP8X4),
                             lhsT_scale=x_scales[:, tokens],
-                            rhs=words[:, i, cols].bitcast(FP8X4),
-                            rhs_scale=planes[4 * (g % SHARED) : P, g // SHARED, cols],
+                            rhs=words[:, j, cols].bitcast(FP8X4),
+                            rhs_scale=planes[4 * j : P, chunk, cols],
                             start=(g == 0),
                             stop=(g == PASSES_1 - 1),
                         )
 
         down_words = []
         for chunk in range(CHUNKS_2):
-            words = ring.tile([P, PASSES_2, CHUNK_COLS], U32, tag="words", align_bytes=64, name="down_words%d" % chunk)
+            words = ring.tile(
+                [P, PASSES_2, DOWN_COLS], U32, tag="words", align_bytes=64, name="down_words%d" % chunk
+            )
             nc.sync.dma_start(
                 out=words[:].bitcast(I32),
-                in_=down_src[:, :, CHUNK_COLS * chunk : CHUNK_COLS * (chunk + 1)],
+                in_=down_src[:, :, DOWN_COLS * chunk : DOWN_COLS * (chunk + 1)],
             )
             down_words.append(words)
 
@@ -198,27 +201,27 @@ def tile_cudaternaryexpertmodule_k_kernel(
             )
 
         for chunk in range(CHUNKS_2):
-            result = results.tile([P, CHUNK_COLS], F32)
-            for h in range(CHUNK_COLS // N_TILE):
-                first = CHUNK_COLS * chunk + N_TILE * h
-                j, n = divmod(first, HIDDEN // SHARED)
+            result = results.tile([P, DOWN_COLS], F32)
+            for h in range(DOWN_COLS // N_TILE):
+                cols = slice(N_TILE * h, N_TILE * (h + 1))
                 acc_out = psum_acc.tile([P, N_TILE], F32, tag="acc")
                 for g in range(PASSES_2):
+                    tokens = slice(P * g, P * (g + 1))
                     nc.tensor.matmul_mx(
                         out=acc_out[:],
-                        lhsT=h_codes[:, P * g : P * (g + 1)].bitcast(FP8X4),
-                        lhsT_scale=h_scales[:, P * g : P * (g + 1)],
-                        rhs=down_words[chunk][:, g, N_TILE * h : N_TILE * (h + 1)].bitcast(FP8X4),
-                        rhs_scale=down_planes[4 * j : P, g, n : n + N_TILE],
+                        lhsT=h_codes[:, tokens].bitcast(FP8X4),
+                        lhsT_scale=h_scales[:, tokens],
+                        rhs=down_words[chunk][:, g, cols].bitcast(FP8X4),
+                        rhs_scale=down_planes[4 * chunk : P, g, cols],
                         start=(g == 0),
                         stop=(g == PASSES_2 - 1),
                     )
                 nc.vector.tensor_tensor(
-                    out=result[:, N_TILE * h : N_TILE * (h + 1)],
+                    out=result[:, cols],
                     in0=acc_out[:],
-                    in1=s_bcast[:, DOWN_ROW + first // N_TILE, :],
+                    in1=s_bcast[:, DOWN_ROW + (DOWN_COLS // N_TILE) * chunk + h, :],
                     op=MULT,
                 )
             nc.sync.dma_start(
-                out=out_rows[:, CHUNK_COLS * chunk : CHUNK_COLS * (chunk + 1)], in_=result[:]
+                out=out_rows[:, DOWN_COLS * chunk : DOWN_COLS * (chunk + 1)], in_=result[:]
             )

@@ -23,7 +23,8 @@ SHARED = 4
 CHUNKS_1 = PASSES_1 // SHARED
 CHUNKS_2 = SHARED
 DOWN_COLS = HIDDEN // CHUNKS_2
-RING = 6
+RING = 7
+STORE_COLS = 1024
 GATE_ROW = 0
 UP_ROW = GATE_ROW + INNER // N_TILE
 DOWN_ROW = UP_ROW + INNER // N_TILE
@@ -64,8 +65,8 @@ def tile_cudaternaryexpertmodule_k_kernel(
     with ExitStack() as ctx:
         keep = ctx.enter_context(tc.tile_pool(name="keep", bufs=1))
         ring = ctx.enter_context(tc.tile_pool(name="ring", bufs=RING))
-        work = ctx.enter_context(tc.tile_pool(name="work", bufs=3))
-        results = ctx.enter_context(tc.tile_pool(name="results", bufs=CHUNKS_2))
+        work = ctx.enter_context(tc.tile_pool(name="work", bufs=2))
+        results = ctx.enter_context(tc.tile_pool(name="results", bufs=HIDDEN // STORE_COLS))
         psum_acc = ctx.enter_context(tc.psum_pool(name="psum_acc", bufs=4))
         psum_aux = ctx.enter_context(tc.psum_pool(name="psum_aux", bufs=4))
 
@@ -124,17 +125,6 @@ def tile_cudaternaryexpertmodule_k_kernel(
             )
 
         s_bcast = keep.tile([P, S_ROWS, N_TILE], BF16)
-        for r in range(S_ROWS):
-            spread = psum_aux.tile([P, N_TILE], F32, tag="aux")
-            nc.tensor.matmul(
-                out=spread[:],
-                lhsT=ident_bf16[:, r : r + 1].to_broadcast([P, P]),
-                rhs=s_rows[:],
-                start=True,
-                stop=True,
-            )
-            nc.scalar.copy(out=s_bcast[:, r, :], in_=spread[:])
-
         acc_gate = [psum_acc.tile([P, N_TILE], F32, tag="acc", name="acc_gate%d" % h) for h in range(2)]
         acc_up = [psum_acc.tile([P, N_TILE], F32, tag="acc", name="acc_up%d" % h) for h in range(2)]
         for chunk in range(CHUNKS_1):
@@ -161,6 +151,18 @@ def tile_cudaternaryexpertmodule_k_kernel(
                             start=(g == 0),
                             stop=(g == PASSES_1 - 1),
                         )
+
+            if chunk == 1:
+                for r in range(S_ROWS):
+                    spread = psum_aux.tile([P, N_TILE], F32, tag="aux")
+                    nc.tensor.matmul(
+                        out=spread[:],
+                        lhsT=ident_bf16[:, r : r + 1].to_broadcast([P, P]),
+                        rhs=s_rows[:],
+                        start=True,
+                        stop=True,
+                    )
+                    nc.scalar.copy(out=s_bcast[:, r, :], in_=spread[:])
 
         down_words = []
         for chunk in range(CHUNKS_2):
@@ -200,10 +202,12 @@ def tile_cudaternaryexpertmodule_k_kernel(
                 in_=h_grouped[:].rearrange("p r t -> p (r t)"),
             )
 
-        for chunk in range(CHUNKS_2):
-            result = results.tile([P, DOWN_COLS], F32)
-            for h in range(DOWN_COLS // N_TILE):
-                cols = slice(N_TILE * h, N_TILE * (h + 1))
+        for part in range(HIDDEN // STORE_COLS):
+            chunk = part * STORE_COLS // DOWN_COLS
+            result = results.tile([P, STORE_COLS], F32)
+            for h in range(STORE_COLS // N_TILE):
+                n0 = STORE_COLS * part + N_TILE * h
+                cols = slice(n0 - DOWN_COLS * chunk, n0 - DOWN_COLS * chunk + N_TILE)
                 acc_out = psum_acc.tile([P, N_TILE], F32, tag="acc")
                 for g in range(PASSES_2):
                     tokens = slice(P * g, P * (g + 1))
@@ -217,11 +221,11 @@ def tile_cudaternaryexpertmodule_k_kernel(
                         stop=(g == PASSES_2 - 1),
                     )
                 nc.vector.tensor_tensor(
-                    out=result[:, cols],
+                    out=result[:, N_TILE * h : N_TILE * (h + 1)],
                     in0=acc_out[:],
-                    in1=s_bcast[:, DOWN_ROW + (DOWN_COLS // N_TILE) * chunk + h, :],
+                    in1=s_bcast[:, DOWN_ROW + n0 // N_TILE, :],
                     op=MULT,
                 )
             nc.sync.dma_start(
-                out=out_rows[:, DOWN_COLS * chunk : DOWN_COLS * (chunk + 1)], in_=result[:]
+                out=out_rows[:, STORE_COLS * part : STORE_COLS * (part + 1)], in_=result[:]
             )

@@ -20,11 +20,14 @@ N_TILE = 512
 PASSES_1 = HIDDEN // K_PASS
 PASSES_2 = INNER // K_PASS
 SHARED = 4
-CHUNKS_1 = PASSES_1 // SHARED
-CHUNKS_2 = SHARED
-DOWN_COLS = HIDDEN // CHUNKS_2
-RING = 7
-STORE_COLS = 1024
+SETS_1 = PASSES_1 // SHARED
+PLANE_COLS = HIDDEN // SHARED
+CHUNK_PASSES = 8
+CHUNKS_1 = PASSES_1 // CHUNK_PASSES
+DOWN_COLS = 4096
+RING = 4
+DOWN_LOADS = (4096, 2048, 2048)
+STORES = (2048, 2048, 2048, 1024, 1024)
 GATE_ROW = 0
 UP_ROW = GATE_ROW + INNER // N_TILE
 DOWN_ROW = UP_ROW + INNER // N_TILE
@@ -66,79 +69,78 @@ def tile_cudaternaryexpertmodule_k_kernel(
         keep = ctx.enter_context(tc.tile_pool(name="keep", bufs=1))
         ring = ctx.enter_context(tc.tile_pool(name="ring", bufs=RING))
         work = ctx.enter_context(tc.tile_pool(name="work", bufs=2))
-        results = ctx.enter_context(tc.tile_pool(name="results", bufs=HIDDEN // STORE_COLS))
         psum_acc = ctx.enter_context(tc.psum_pool(name="psum_acc", bufs=4))
         psum_aux = ctx.enter_context(tc.psum_pool(name="psum_aux", bufs=4))
 
-        x_sb = keep.tile([P, HIDDEN], BF16)
-        for half in range(2):
-            cols = slice(half * HIDDEN // 2, (half + 1) * HIDDEN // 2)
-            nc.sync.dma_start(out=x_sb[:, cols], in_=x_rows[:, cols])
+        with tc.tile_pool(name="head", bufs=1) as head_pool:
+            x_sb = head_pool.tile([P, HIDDEN], BF16)
+            nc.sync.dma_start(out=x_sb[:], in_=x_rows)
 
-        ident_f32 = keep.tile([P, P], F32)
-        make_identity(nc, ident_f32[:])
-        ident_bf16 = keep.tile([P, P], BF16)
-        make_identity(nc, ident_bf16[:])
+            ident_f32 = keep.tile([P, P], F32)
+            make_identity(nc, ident_f32[:])
+            ident_bf16 = keep.tile([P, P], BF16)
+            make_identity(nc, ident_bf16[:])
 
-        gate_planes = keep.tile([P, CHUNKS_1, INNER], U8, align_bytes=64)
-        up_planes = keep.tile([P, CHUNKS_1, INNER], U8, align_bytes=64)
-        down_planes = keep.tile([P, PASSES_2, DOWN_COLS], U8, align_bytes=64)
-        for planes in (gate_planes, up_planes, down_planes):
-            nc.vector.memset(planes[:].bitcast(I32), 0)
+            gate_planes = keep.tile([P, SETS_1, INNER], U8, align_bytes=64)
+            up_planes = keep.tile([P, SETS_1, INNER], U8, align_bytes=64)
+            down_planes = keep.tile([P, PASSES_2, PLANE_COLS], U8, align_bytes=64)
+            for planes in (gate_planes, up_planes, down_planes):
+                nc.vector.memset(planes[:].bitcast(I32), 0)
 
-        for chunk in range(CHUNKS_1):
-            for planes, scales in ((gate_planes, gate_w_scales), (up_planes, up_w_scales)):
-                load_shared_planes(
-                    nc, planes[:, chunk, :], scales[SHARED * chunk : SHARED * (chunk + 1), :, :]
-                )
-        for g in range(PASSES_2):
-            load_shared_planes(
-                nc, down_planes[:, g, :], down_w_scales[g].rearrange("q (j n) -> j q n", j=SHARED)
-            )
-
-        s_rows = keep.tile([P, N_TILE], BF16)
-        nc.vector.memset(s_rows[:], 0.0)
-        nc.scalar.dma_start(out=s_rows[GATE_ROW:UP_ROW, :], in_=gate_s.rearrange("(r c) -> r c", c=N_TILE))
-        nc.scalar.dma_start(out=s_rows[UP_ROW:DOWN_ROW, :], in_=up_s.rearrange("(r c) -> r c", c=N_TILE))
-        nc.scalar.dma_start(out=s_rows[DOWN_ROW:S_ROWS, :], in_=down_s.rearrange("(r c) -> r c", c=N_TILE))
-
-        x_codes = keep.tile([P, PASSES_1 * P], U32, align_bytes=64)
-        x_scales = keep.tile([P, PASSES_1 * P], U8, align_bytes=64)
-        x_words = x_sb[:].bitcast(F32)
-        for pair in range(PASSES_1 // 2):
-            xt = psum_aux.tile([P, 2, 2, P], F32, tag="aux")
-            for i in range(2):
-                g = 2 * pair + i
-                for u in range(2):
-                    nc.tensor.transpose(
-                        xt[:, i, u, :], x_words[:, 256 * g + u : 256 * (g + 1) : 2], ident_f32[:]
+            for c in range(SETS_1):
+                for planes, scales in ((gate_planes, gate_w_scales), (up_planes, up_w_scales)):
+                    load_shared_planes(
+                        nc, planes[:, c, :], scales[SHARED * c : SHARED * (c + 1), :, :]
                     )
-            x_grouped = work.tile([P, 2 * K_PASS], BF16, align_bytes=64)
-            grouped_words = x_grouped[:].bitcast(F32).rearrange("p (i r u) -> p i r u", i=2, u=2)
-            if pair % 2 == 0:
-                nc.vector.tensor_copy(out=grouped_words, in_=xt[:].rearrange("p i u r -> p i r u"))
-            else:
-                nc.scalar.copy(out=grouped_words, in_=xt[:].rearrange("p i u r -> p i r u"))
-            cols = slice(2 * P * pair, 2 * P * (pair + 1))
-            nc.vector.quantize_mx(
-                out=x_codes[:, cols].bitcast(FP8X4), scales=x_scales[:, cols], in_=x_grouped[:]
-            )
+            for g in range(PASSES_2):
+                load_shared_planes(
+                    nc, down_planes[:, g, :], down_w_scales[g].rearrange("q (j n) -> j q n", j=SHARED)
+                )
+
+            s_rows = keep.tile([P, N_TILE], BF16)
+            nc.vector.memset(s_rows[:], 0.0)
+            nc.scalar.dma_start(out=s_rows[GATE_ROW:UP_ROW, :], in_=gate_s.rearrange("(r c) -> r c", c=N_TILE))
+            nc.scalar.dma_start(out=s_rows[UP_ROW:DOWN_ROW, :], in_=up_s.rearrange("(r c) -> r c", c=N_TILE))
+            nc.scalar.dma_start(out=s_rows[DOWN_ROW:S_ROWS, :], in_=down_s.rearrange("(r c) -> r c", c=N_TILE))
+
+            x_codes = keep.tile([P, PASSES_1 * P], U32, align_bytes=64)
+            x_scales = keep.tile([P, PASSES_1 * P], U8, align_bytes=64)
+            x_words = x_sb[:].bitcast(F32)
+            for pair in range(PASSES_1 // 2):
+                xt = psum_aux.tile([P, 2, 2, P], F32, tag="aux")
+                for i in range(2):
+                    g = 2 * pair + i
+                    for u in range(2):
+                        nc.tensor.transpose(
+                            xt[:, i, u, :], x_words[:, 256 * g + u : 256 * (g + 1) : 2], ident_f32[:]
+                        )
+                x_grouped = work.tile([P, 2 * K_PASS], BF16, align_bytes=64)
+                grouped_words = x_grouped[:].bitcast(F32).rearrange("p (i r u) -> p i r u", i=2, u=2)
+                if pair % 2 == 0:
+                    nc.vector.tensor_copy(out=grouped_words, in_=xt[:].rearrange("p i u r -> p i r u"))
+                else:
+                    nc.scalar.copy(out=grouped_words, in_=xt[:].rearrange("p i u r -> p i r u"))
+                cols = slice(2 * P * pair, 2 * P * (pair + 1))
+                nc.vector.quantize_mx(
+                    out=x_codes[:, cols].bitcast(FP8X4), scales=x_scales[:, cols], in_=x_grouped[:]
+                )
+        results = ctx.enter_context(tc.tile_pool(name="results", bufs=len(STORES)))
 
         s_bcast = keep.tile([P, S_ROWS, N_TILE], BF16)
         acc_gate = [psum_acc.tile([P, N_TILE], F32, tag="acc", name="acc_gate%d" % h) for h in range(2)]
         acc_up = [psum_acc.tile([P, N_TILE], F32, tag="acc", name="acc_up%d" % h) for h in range(2)]
         for chunk in range(CHUNKS_1):
-            passes = slice(SHARED * chunk, SHARED * (chunk + 1))
-            gate_words = ring.tile([P, SHARED, INNER], U32, tag="words", align_bytes=64)
+            passes = slice(CHUNK_PASSES * chunk, CHUNK_PASSES * (chunk + 1))
+            gate_words = ring.tile([P, CHUNK_PASSES, INNER], U32, tag="words", align_bytes=64)
             nc.sync.dma_start(out=gate_words[:].bitcast(I32), in_=gate_src[:, passes, :])
-            up_words = ring.tile([P, SHARED, INNER], U32, tag="words", align_bytes=64)
+            up_words = ring.tile([P, CHUNK_PASSES, INNER], U32, tag="words", align_bytes=64)
             nc.sync.dma_start(out=up_words[:].bitcast(I32), in_=up_src[:, passes, :])
             for acc, words, planes in (
                 (acc_gate, gate_words, gate_planes),
                 (acc_up, up_words, up_planes),
             ):
-                for j in range(SHARED):
-                    g = SHARED * chunk + j
+                for j in range(CHUNK_PASSES):
+                    g = CHUNK_PASSES * chunk + j
                     tokens = slice(P * g, P * (g + 1))
                     for h in range(INNER // N_TILE):
                         cols = slice(N_TILE * h, N_TILE * (h + 1))
@@ -147,12 +149,12 @@ def tile_cudaternaryexpertmodule_k_kernel(
                             lhsT=x_codes[:, tokens].bitcast(FP8X4),
                             lhsT_scale=x_scales[:, tokens],
                             rhs=words[:, j, cols].bitcast(FP8X4),
-                            rhs_scale=planes[4 * j : P, chunk, cols],
+                            rhs_scale=planes[4 * (g % SHARED) : P, g // SHARED, cols],
                             start=(g == 0),
                             stop=(g == PASSES_1 - 1),
                         )
 
-            if chunk == 1:
+            if chunk == 0:
                 for r in range(S_ROWS):
                     spread = psum_aux.tile([P, N_TILE], F32, tag="aux")
                     nc.tensor.matmul(
@@ -165,15 +167,19 @@ def tile_cudaternaryexpertmodule_k_kernel(
                     nc.scalar.copy(out=s_bcast[:, r, :], in_=spread[:])
 
         down_words = []
-        for chunk in range(CHUNKS_2):
+        for chunk in range(HIDDEN // DOWN_COLS):
             words = ring.tile(
                 [P, PASSES_2, DOWN_COLS], U32, tag="words", align_bytes=64, name="down_words%d" % chunk
             )
-            nc.sync.dma_start(
-                out=words[:].bitcast(I32),
-                in_=down_src[:, :, DOWN_COLS * chunk : DOWN_COLS * (chunk + 1)],
-            )
             down_words.append(words)
+        n0 = 0
+        for width in DOWN_LOADS:
+            start = n0 % DOWN_COLS
+            nc.sync.dma_start(
+                out=down_words[n0 // DOWN_COLS][:, :, start : start + width].bitcast(I32),
+                in_=down_src[:, :, n0 : n0 + width],
+            )
+            n0 += width
 
         hdn = keep.tile([P, INNER], BF16)
         h_codes = keep.tile([P, PASSES_2 * P], U32, align_bytes=64)
@@ -202,12 +208,11 @@ def tile_cudaternaryexpertmodule_k_kernel(
                 in_=h_grouped[:].rearrange("p r t -> p (r t)"),
             )
 
-        for part in range(HIDDEN // STORE_COLS):
-            chunk = part * STORE_COLS // DOWN_COLS
-            result = results.tile([P, STORE_COLS], F32)
-            for h in range(STORE_COLS // N_TILE):
-                n0 = STORE_COLS * part + N_TILE * h
-                cols = slice(n0 - DOWN_COLS * chunk, n0 - DOWN_COLS * chunk + N_TILE)
+        n0 = 0
+        for width in STORES:
+            result = results.tile([P, width], F32)
+            for h in range(width // N_TILE):
+                start = n0 % DOWN_COLS
                 acc_out = psum_acc.tile([P, N_TILE], F32, tag="acc")
                 for g in range(PASSES_2):
                     tokens = slice(P * g, P * (g + 1))
@@ -215,8 +220,10 @@ def tile_cudaternaryexpertmodule_k_kernel(
                         out=acc_out[:],
                         lhsT=h_codes[:, tokens].bitcast(FP8X4),
                         lhsT_scale=h_scales[:, tokens],
-                        rhs=down_words[chunk][:, g, cols].bitcast(FP8X4),
-                        rhs_scale=down_planes[4 * chunk : P, g, cols],
+                        rhs=down_words[n0 // DOWN_COLS][:, g, start : start + N_TILE].bitcast(FP8X4),
+                        rhs_scale=down_planes[
+                            4 * (n0 // PLANE_COLS) : P, g, n0 % PLANE_COLS : n0 % PLANE_COLS + N_TILE
+                        ],
                         start=(g == 0),
                         stop=(g == PASSES_2 - 1),
                     )
@@ -226,6 +233,5 @@ def tile_cudaternaryexpertmodule_k_kernel(
                     in1=s_bcast[:, DOWN_ROW + n0 // N_TILE, :],
                     op=MULT,
                 )
-            nc.sync.dma_start(
-                out=out_rows[:, STORE_COLS * part : STORE_COLS * (part + 1)], in_=result[:]
-            )
+                n0 += N_TILE
+            nc.sync.dma_start(out=out_rows[:, n0 - width : n0], in_=result[:])

@@ -27,7 +27,7 @@ CHUNKS_1 = PASSES_1 // CHUNK_PASSES
 DOWN_COLS = 4096
 RING = 4
 DOWN_LOADS = (4096, 2048, 2048)
-STORES = (2048, 2048, 2048, 1024, 1024)
+STORES = (2048, 2048, 2048, 2048)
 GATE_ROW = 0
 UP_ROW = GATE_ROW + INNER // N_TILE
 DOWN_ROW = UP_ROW + INNER // N_TILE
@@ -71,6 +71,7 @@ def tile_cudaternaryexpertmodule_k_kernel(
         work = ctx.enter_context(tc.tile_pool(name="work", bufs=2))
         psum_acc = ctx.enter_context(tc.psum_pool(name="psum_acc", bufs=4))
         psum_aux = ctx.enter_context(tc.psum_pool(name="psum_aux", bufs=4))
+        ctx.enter_context(tc.manual_schedule())
 
         with tc.tile_pool(name="head", bufs=1) as head_pool:
             x_sb = head_pool.tile([P, HIDDEN], BF16)

@@ -26,8 +26,10 @@ CHUNK_PASSES = 8
 CHUNKS_1 = PASSES_1 // CHUNK_PASSES
 DOWN_COLS = 4096
 RING = 4
-DOWN_LOADS = (4096, 2048, 2048)
-STORES = (2048, 2048, 2048, 2048)
+DOWN_LOADS = (2048, 2048, 2048, 2048)
+STORES = (2048, 2048, 2048, 1024, 1024)
+GATE_LOADS = ((8,), (8,))
+UP_LOADS = ((8,), (6, 2))
 GATE_ROW = 0
 UP_ROW = GATE_ROW + INNER // N_TILE
 DOWN_ROW = UP_ROW + INNER // N_TILE
@@ -42,6 +44,11 @@ def load_shared_planes(nc, planes, scale_rows):
             out=planes[32 * quadrant : 32 * quadrant + 4 * SHARED, :].bitcast(F32),
             in_=scale_rows[:, 4 * quadrant : 4 * quadrant + 4, :].bitcast(F32),
         )
+
+
+def quantise_pair(nc, codes, scales, pair, grouped):
+    cols = slice(2 * P * pair, 2 * P * (pair + 1))
+    nc.vector.quantize_mx(out=codes[:, cols].bitcast(FP8X4), scales=scales[:, cols], in_=grouped[:])
 
 
 def tile_cudaternaryexpertmodule_k_kernel(
@@ -68,7 +75,7 @@ def tile_cudaternaryexpertmodule_k_kernel(
     with ExitStack() as ctx:
         keep = ctx.enter_context(tc.tile_pool(name="keep", bufs=1))
         ring = ctx.enter_context(tc.tile_pool(name="ring", bufs=RING))
-        work = ctx.enter_context(tc.tile_pool(name="work", bufs=2))
+        work = ctx.enter_context(tc.tile_pool(name="work", bufs=3))
         psum_acc = ctx.enter_context(tc.psum_pool(name="psum_acc", bufs=4))
         psum_aux = ctx.enter_context(tc.psum_pool(name="psum_aux", bufs=4))
         ctx.enter_context(tc.manual_schedule())
@@ -85,6 +92,8 @@ def tile_cudaternaryexpertmodule_k_kernel(
             gate_planes = keep.tile([P, SETS_1, INNER], U8, align_bytes=64)
             up_planes = keep.tile([P, SETS_1, INNER], U8, align_bytes=64)
             down_planes = keep.tile([P, PASSES_2, PLANE_COLS], U8, align_bytes=64)
+            s_rows = keep.tile([P, N_TILE], BF16)
+            nc.vector.memset(s_rows[:], 0.0)
             for planes in (gate_planes, up_planes, down_planes):
                 nc.vector.memset(planes[:].bitcast(I32), 0)
 
@@ -98,8 +107,6 @@ def tile_cudaternaryexpertmodule_k_kernel(
                     nc, down_planes[:, g, :], down_w_scales[g].rearrange("q (j n) -> j q n", j=SHARED)
                 )
 
-            s_rows = keep.tile([P, N_TILE], BF16)
-            nc.vector.memset(s_rows[:], 0.0)
             nc.scalar.dma_start(out=s_rows[GATE_ROW:UP_ROW, :], in_=gate_s.rearrange("(r c) -> r c", c=N_TILE))
             nc.scalar.dma_start(out=s_rows[UP_ROW:DOWN_ROW, :], in_=up_s.rearrange("(r c) -> r c", c=N_TILE))
             nc.scalar.dma_start(out=s_rows[DOWN_ROW:S_ROWS, :], in_=down_s.rearrange("(r c) -> r c", c=N_TILE))
@@ -107,6 +114,7 @@ def tile_cudaternaryexpertmodule_k_kernel(
             x_codes = keep.tile([P, PASSES_1 * P], U32, align_bytes=64)
             x_scales = keep.tile([P, PASSES_1 * P], U8, align_bytes=64)
             x_words = x_sb[:].bitcast(F32)
+            groups = []
             for pair in range(PASSES_1 // 2):
                 xt = psum_aux.tile([P, 2, 2, P], F32, tag="aux")
                 for i in range(2):
@@ -121,39 +129,42 @@ def tile_cudaternaryexpertmodule_k_kernel(
                     nc.vector.tensor_copy(out=grouped_words, in_=xt[:].rearrange("p i u r -> p i r u"))
                 else:
                     nc.scalar.copy(out=grouped_words, in_=xt[:].rearrange("p i u r -> p i r u"))
-                cols = slice(2 * P * pair, 2 * P * (pair + 1))
-                nc.vector.quantize_mx(
-                    out=x_codes[:, cols].bitcast(FP8X4), scales=x_scales[:, cols], in_=x_grouped[:]
-                )
+                groups.append(x_grouped)
+                if pair > 0:
+                    quantise_pair(nc, x_codes, x_scales, pair - 1, groups[pair - 1])
+            quantise_pair(nc, x_codes, x_scales, len(groups) - 1, groups[-1])
         results = ctx.enter_context(tc.tile_pool(name="results", bufs=len(STORES)))
 
         s_bcast = keep.tile([P, S_ROWS, N_TILE], BF16)
         acc_gate = [psum_acc.tile([P, N_TILE], F32, tag="acc", name="acc_gate%d" % h) for h in range(2)]
         acc_up = [psum_acc.tile([P, N_TILE], F32, tag="acc", name="acc_up%d" % h) for h in range(2)]
         for chunk in range(CHUNKS_1):
-            passes = slice(CHUNK_PASSES * chunk, CHUNK_PASSES * (chunk + 1))
             gate_words = ring.tile([P, CHUNK_PASSES, INNER], U32, tag="words", align_bytes=64)
-            nc.sync.dma_start(out=gate_words[:].bitcast(I32), in_=gate_src[:, passes, :])
             up_words = ring.tile([P, CHUNK_PASSES, INNER], U32, tag="words", align_bytes=64)
-            nc.sync.dma_start(out=up_words[:].bitcast(I32), in_=up_src[:, passes, :])
-            for acc, words, planes in (
-                (acc_gate, gate_words, gate_planes),
-                (acc_up, up_words, up_planes),
+            for acc, words, planes, source, loads in (
+                (acc_gate, gate_words, gate_planes, gate_src, GATE_LOADS[chunk]),
+                (acc_up, up_words, up_planes, up_src, UP_LOADS[chunk]),
             ):
-                for j in range(CHUNK_PASSES):
-                    g = CHUNK_PASSES * chunk + j
-                    tokens = slice(P * g, P * (g + 1))
+                j0 = 0
+                for count in loads:
+                    g0 = CHUNK_PASSES * chunk + j0
+                    nc.sync.dma_start(
+                        out=words[:, j0 : j0 + count, :].bitcast(I32), in_=source[:, g0 : g0 + count, :]
+                    )
                     for h in range(INNER // N_TILE):
                         cols = slice(N_TILE * h, N_TILE * (h + 1))
-                        nc.tensor.matmul_mx(
-                            out=acc[h][:],
-                            lhsT=x_codes[:, tokens].bitcast(FP8X4),
-                            lhsT_scale=x_scales[:, tokens],
-                            rhs=words[:, j, cols].bitcast(FP8X4),
-                            rhs_scale=planes[4 * (g % SHARED) : P, g // SHARED, cols],
-                            start=(g == 0),
-                            stop=(g == PASSES_1 - 1),
-                        )
+                        for g in range(g0, g0 + count):
+                            tokens = slice(P * g, P * (g + 1))
+                            nc.tensor.matmul_mx(
+                                out=acc[h][:],
+                                lhsT=x_codes[:, tokens].bitcast(FP8X4),
+                                lhsT_scale=x_scales[:, tokens],
+                                rhs=words[:, g - CHUNK_PASSES * chunk, cols].bitcast(FP8X4),
+                                rhs_scale=planes[4 * (g % SHARED) : P, g // SHARED, cols],
+                                start=(g == 0),
+                                stop=(g == PASSES_1 - 1),
+                            )
+                    j0 += count
 
             if chunk == 0:
                 for r in range(S_ROWS):
@@ -165,7 +176,10 @@ def tile_cudaternaryexpertmodule_k_kernel(
                         start=True,
                         stop=True,
                     )
-                    nc.scalar.copy(out=s_bcast[:, r, :], in_=spread[:])
+                    if r % 2 == 0:
+                        nc.vector.tensor_copy(out=s_bcast[:, r, :], in_=spread[:])
+                    else:
+                        nc.scalar.copy(out=s_bcast[:, r, :], in_=spread[:])
 
         down_words = []
         for chunk in range(HIDDEN // DOWN_COLS):
@@ -182,31 +196,38 @@ def tile_cudaternaryexpertmodule_k_kernel(
             )
             n0 += width
 
+        halves = range(PASSES_2)
+        gate_f = [keep.tile([P, N_TILE], F32, name="gate_f%d" % g) for g in halves]
+        silu_f = [keep.tile([P, N_TILE], F32, name="silu_f%d" % g) for g in halves]
+        factor = [keep.tile([P, N_TILE], F32, name="factor%d" % g) for g in halves]
+        for g in halves:
+            nc.vector.tensor_tensor(out=gate_f[g][:], in0=acc_gate[g][:], in1=s_bcast[:, GATE_ROW + g, :], op=MULT)
+            nc.scalar.activation(out=silu_f[g][:], in_=gate_f[g][:], func=SILU)
+        for g in halves:
+            nc.vector.tensor_tensor(out=factor[g][:], in0=silu_f[g][:], in1=s_bcast[:, UP_ROW + g, :], op=MULT)
+
         hdn = keep.tile([P, INNER], BF16)
         h_codes = keep.tile([P, PASSES_2 * P], U32, align_bytes=64)
         h_scales = keep.tile([P, PASSES_2 * P], U8, align_bytes=64)
-        for g in range(PASSES_2):
-            gate_f = work.tile([P, N_TILE], F32)
-            nc.vector.tensor_tensor(out=gate_f[:], in0=acc_gate[g][:], in1=s_bcast[:, GATE_ROW + g, :], op=MULT)
-            silu_f = work.tile([P, N_TILE], F32)
-            nc.scalar.activation(out=silu_f[:], in_=gate_f[:], func=SILU)
-            up_f = work.tile([P, N_TILE], F32)
-            nc.vector.tensor_tensor(out=up_f[:], in0=acc_up[g][:], in1=s_bcast[:, UP_ROW + g, :], op=MULT)
+        h_grouped = []
+        for g in halves:
             nc.vector.tensor_tensor(
-                out=hdn[:, K_PASS * g : K_PASS * (g + 1)], in0=silu_f[:], in1=up_f[:], op=MULT
+                out=hdn[:, K_PASS * g : K_PASS * (g + 1)], in0=acc_up[g][:], in1=factor[g][:], op=MULT
             )
             ht = psum_aux.tile([P, 4, P], BF16, tag="aux")
             for t in range(4):
                 nc.tensor.transpose(
                     ht[:, t, :], hdn[:, K_PASS * g + t : K_PASS * (g + 1) : 4], ident_bf16[:]
                 )
-            h_grouped = work.tile([P, P, 4], BF16, align_bytes=64)
-            nc.scalar.copy(out=h_grouped[:], in_=ht[:].rearrange("p t r -> p r t"))
+            grouped = work.tile([P, P, 4], BF16, align_bytes=64)
+            nc.scalar.copy(out=grouped[:], in_=ht[:].rearrange("p t r -> p r t"))
+            h_grouped.append(grouped)
+        for g in halves:
             tokens = slice(P * g, P * (g + 1))
             nc.vector.quantize_mx(
                 out=h_codes[:, tokens].bitcast(FP8X4),
                 scales=h_scales[:, tokens],
-                in_=h_grouped[:].rearrange("p r t -> p (r t)"),
+                in_=h_grouped[g][:].rearrange("p r t -> p (r t)"),
             )
 
         n0 = 0

@@ -26,8 +26,8 @@ CHUNK_PASSES = 8
 CHUNKS_1 = PASSES_1 // CHUNK_PASSES
 DOWN_COLS = 4096
 RING = 4
-DOWN_LOADS = (2048, 2048, 2048, 2048)
-STORES = (2048, 2048, 2048, 1024, 1024)
+DOWN_LOADS = (4096, 2048, 2048)
+STORES = (4096, 2048, 1024, 1024)
 GATE_LOADS = ((8,), (8,))
 UP_LOADS = ((8,), (6, 2))
 GATE_ROW = 0
@@ -133,7 +133,7 @@ def tile_cudaternaryexpertmodule_k_kernel(
                 if pair > 0:
                     quantise_pair(nc, x_codes, x_scales, pair - 1, groups[pair - 1])
             quantise_pair(nc, x_codes, x_scales, len(groups) - 1, groups[-1])
-        results = ctx.enter_context(tc.tile_pool(name="results", bufs=len(STORES)))
+        results = ctx.enter_context(tc.tile_pool(name="results", bufs=1))
 
         s_bcast = keep.tile([P, S_ROWS, N_TILE], BF16)
         acc_gate = [psum_acc.tile([P, N_TILE], F32, tag="acc", name="acc_gate%d" % h) for h in range(2)]
@@ -231,8 +231,8 @@ def tile_cudaternaryexpertmodule_k_kernel(
             )
 
         n0 = 0
-        for width in STORES:
-            result = results.tile([P, width], F32)
+        for i, width in enumerate(STORES):
+            result = results.tile([P, width], F32, name="result%d" % i)
             for h in range(width // N_TILE):
                 start = n0 % DOWN_COLS
                 acc_out = psum_acc.tile([P, N_TILE], F32, tag="acc")

from contextlib import ExitStack

import concourse.mybir as mybir
from concourse.masks import make_identity

F32 = mybir.dt.float32
BF16 = mybir.dt.bfloat16
I32 = mybir.dt.int32
U32 = mybir.dt.uint32
U8 = mybir.dt.uint8
FP8X4 = mybir.dt.float8_e4m3fn_x4
MULT = mybir.AluOpType.mult
SILU = mybir.ActivationFunctionType.Silu

P = 128
HIDDEN = 8192
INNER = 1024
K_PASS = 512
N_TILE = 512
PASSES_1 = HIDDEN // K_PASS
PASSES_2 = INNER // K_PASS
SHARED = 4
SETS_1 = PASSES_1 // SHARED
PLANE_COLS = HIDDEN // SHARED
CHUNK_PASSES = 8
CHUNKS_1 = PASSES_1 // CHUNK_PASSES
DOWN_COLS = 4096
RING = 4
DOWN_LOADS = (4096, 2048, 2048)
STORES = (4096, 2048, 1024, 1024)
GATE_LOADS = ((8,), (8,))
UP_LOADS = ((8,), (6, 2))
GATE_ROW = 0
UP_ROW = GATE_ROW + INNER // N_TILE
DOWN_ROW = UP_ROW + INNER // N_TILE
S_ROWS = DOWN_ROW + HIDDEN // N_TILE

FLOPS = 2 * P * HIDDEN * INNER * 3


def load_shared_planes(nc, planes, scale_rows):
    for quadrant in range(4):
        nc.gpsimd.dma_start(
            out=planes[32 * quadrant : 32 * quadrant + 4 * SHARED, :].bitcast(F32),
            in_=scale_rows[:, 4 * quadrant : 4 * quadrant + 4, :].bitcast(F32),
        )


def quantise_pair(nc, codes, scales, pair, grouped):
    cols = slice(2 * P * pair, 2 * P * (pair + 1))
    nc.vector.quantize_mx(out=codes[:, cols].bitcast(FP8X4), scales=scales[:, cols], in_=grouped[:])


def tile_cudaternaryexpertmodule_k_kernel(
    tc,
    x,
    gate_w_words,
    gate_w_scales,
    up_w_words,
    up_w_scales,
    down_w_words,
    down_w_scales,
    gate_s,
    up_s,
    down_s,
    out,
):
    nc = tc.nc
    x_rows = x.flatten_outer_dims()
    out_rows = out.flatten_outer_dims()
    gate_src = gate_w_words.rearrange("g p n t -> p g (n t)").bitcast(I32)
    up_src = up_w_words.rearrange("g p n t -> p g (n t)").bitcast(I32)
    down_src = down_w_words.rearrange("g p n t -> p g (n t)").bitcast(I32)

    with ExitStack() as ctx:
        keep = ctx.enter_context(tc.tile_pool(name="keep", bufs=1))
        ring = ctx.enter_context(tc.tile_pool(name="ring", bufs=RING))
        work = ctx.enter_context(tc.tile_pool(name="work", bufs=3))
        psum_acc = ctx.enter_context(tc.psum_pool(name="psum_acc", bufs=4))
        psum_aux = ctx.enter_context(tc.psum_pool(name="psum_aux", bufs=4))
        ctx.enter_context(tc.manual_schedule())

        with tc.tile_pool(name="head", bufs=1) as head_pool:
            x_sb = head_pool.tile([P, HIDDEN], BF16)
            nc.sync.dma_start(out=x_sb[:], in_=x_rows)

            ident_f32 = keep.tile([P, P], F32)
            make_identity(nc, ident_f32[:])
            ident_bf16 = keep.tile([P, P], BF16)
            make_identity(nc, ident_bf16[:])

            gate_planes = keep.tile([P, SETS_1, INNER], U8, align_bytes=64)
            up_planes = keep.tile([P, SETS_1, INNER], U8, align_bytes=64)
            down_planes = keep.tile([P, PASSES_2, PLANE_COLS], U8, align_bytes=64)
            s_rows = keep.tile([P, N_TILE], BF16)
            nc.vector.memset(s_rows[:], 0.0)
            for planes in (gate_planes, up_planes, down_planes):
                nc.vector.memset(planes[:].bitcast(I32), 0)

            for c in range(SETS_1):
                for planes, scales in ((gate_planes, gate_w_scales), (up_planes, up_w_scales)):
                    load_shared_planes(
                        nc, planes[:, c, :], scales[SHARED * c : SHARED * (c + 1), :, :]
                    )
            for g in range(PASSES_2):
                load_shared_planes(
                    nc, down_planes[:, g, :], down_w_scales[g].rearrange("q (j n) -> j q n", j=SHARED)
                )

            nc.scalar.dma_start(out=s_rows[GATE_ROW:UP_ROW, :], in_=gate_s.rearrange("(r c) -> r c", c=N_TILE))
            nc.scalar.dma_start(out=s_rows[UP_ROW:DOWN_ROW, :], in_=up_s.rearrange("(r c) -> r c", c=N_TILE))
            nc.scalar.dma_start(out=s_rows[DOWN_ROW:S_ROWS, :], in_=down_s.rearrange("(r c) -> r c", c=N_TILE))

            x_codes = keep.tile([P, PASSES_1 * P], U32, align_bytes=64)
            x_scales = keep.tile([P, PASSES_1 * P], U8, align_bytes=64)
            x_words = x_sb[:].bitcast(F32)
            groups = []
            for pair in range(PASSES_1 // 2):
                xt = psum_aux.tile([P, 2, 2, P], F32, tag="aux")
                for i in range(2):
                    g = 2 * pair + i
                    for u in range(2):
                        nc.tensor.transpose(
                            xt[:, i, u, :], x_words[:, 256 * g + u : 256 * (g + 1) : 2], ident_f32[:]
                        )
                x_grouped = work.tile([P, 2 * K_PASS], BF16, align_bytes=64)
                grouped_words = x_grouped[:].bitcast(F32).rearrange("p (i r u) -> p i r u", i=2, u=2)
                if pair % 2 == 0:
                    nc.vector.tensor_copy(out=grouped_words, in_=xt[:].rearrange("p i u r -> p i r u"))
                else:
                    nc.scalar.copy(out=grouped_words, in_=xt[:].rearrange("p i u r -> p i r u"))
                groups.append(x_grouped)
                if pair > 0:
                    quantise_pair(nc, x_codes, x_scales, pair - 1, groups[pair - 1])
            quantise_pair(nc, x_codes, x_scales, len(groups) - 1, groups[-1])
        results = ctx.enter_context(tc.tile_pool(name="results", bufs=1))

        s_bcast = keep.tile([P, S_ROWS, N_TILE], BF16)
        acc_gate = [psum_acc.tile([P, N_TILE], F32, tag="acc", name="acc_gate%d" % h) for h in range(2)]
        acc_up = [psum_acc.tile([P, N_TILE], F32, tag="acc", name="acc_up%d" % h) for h in range(2)]
        for chunk in range(CHUNKS_1):
            gate_words = ring.tile([P, CHUNK_PASSES, INNER], U32, tag="words", align_bytes=64)
            up_words = ring.tile([P, CHUNK_PASSES, INNER], U32, tag="words", align_bytes=64)
            for acc, words, planes, source, loads in (
                (acc_gate, gate_words, gate_planes, gate_src, GATE_LOADS[chunk]),
                (acc_up, up_words, up_planes, up_src, UP_LOADS[chunk]),
            ):
                j0 = 0
                for count in loads:
                    g0 = CHUNK_PASSES * chunk + j0
                    nc.sync.dma_start(
                        out=words[:, j0 : j0 + count, :].bitcast(I32), in_=source[:, g0 : g0 + count, :]
                    )
                    for h in range(INNER // N_TILE):
                        cols = slice(N_TILE * h, N_TILE * (h + 1))
                        for g in range(g0, g0 + count):
                            tokens = slice(P * g, P * (g + 1))
                            nc.tensor.matmul_mx(
                                out=acc[h][:],
                                lhsT=x_codes[:, tokens].bitcast(FP8X4),
                                lhsT_scale=x_scales[:, tokens],
                                rhs=words[:, g - CHUNK_PASSES * chunk, cols].bitcast(FP8X4),
                                rhs_scale=planes[4 * (g % SHARED) : P, g // SHARED, cols],
                                start=(g == 0),
                                stop=(g == PASSES_1 - 1),
                            )
                    j0 += count

            if chunk == 0:
                for r in range(S_ROWS):
                    spread = psum_aux.tile([P, N_TILE], F32, tag="aux")
                    nc.tensor.matmul(
                        out=spread[:],
                        lhsT=ident_bf16[:, r : r + 1].to_broadcast([P, P]),
                        rhs=s_rows[:],
                        start=True,
                        stop=True,
                    )
                    if r % 2 == 0:
                        nc.vector.tensor_copy(out=s_bcast[:, r, :], in_=spread[:])
                    else:
                        nc.scalar.copy(out=s_bcast[:, r, :], in_=spread[:])

        down_words = []
        for chunk in range(HIDDEN // DOWN_COLS):
            words = ring.tile(
                [P, PASSES_2, DOWN_COLS], U32, tag="words", align_bytes=64, name="down_words%d" % chunk
            )
            down_words.append(words)
        n0 = 0
        for width in DOWN_LOADS:
            start = n0 % DOWN_COLS
            nc.sync.dma_start(
                out=down_words[n0 // DOWN_COLS][:, :, start : start + width].bitcast(I32),
                in_=down_src[:, :, n0 : n0 + width],
            )
            n0 += width

        halves = range(PASSES_2)
        gate_f = [keep.tile([P, N_TILE], F32, name="gate_f%d" % g) for g in halves]
        silu_f = [keep.tile([P, N_TILE], F32, name="silu_f%d" % g) for g in halves]
        factor = [keep.tile([P, N_TILE], F32, name="factor%d" % g) for g in halves]
        for g in halves:
            nc.vector.tensor_tensor(out=gate_f[g][:], in0=acc_gate[g][:], in1=s_bcast[:, GATE_ROW + g, :], op=MULT)
            nc.scalar.activation(out=silu_f[g][:], in_=gate_f[g][:], func=SILU)
        for g in halves:
            nc.vector.tensor_tensor(out=factor[g][:], in0=silu_f[g][:], in1=s_bcast[:, UP_ROW + g, :], op=MULT)

        hdn = keep.tile([P, INNER], BF16)
        h_codes = keep.tile([P, PASSES_2 * P], U32, align_bytes=64)
        h_scales = keep.tile([P, PASSES_2 * P], U8, align_bytes=64)
        h_grouped = []
        for g in halves:
            nc.vector.tensor_tensor(
                out=hdn[:, K_PASS * g : K_PASS * (g + 1)], in0=acc_up[g][:], in1=factor[g][:], op=MULT
            )
            ht = psum_aux.tile([P, 4, P], BF16, tag="aux")
            for t in range(4):
                nc.tensor.transpose(
                    ht[:, t, :], hdn[:, K_PASS * g + t : K_PASS * (g + 1) : 4], ident_bf16[:]
                )
            grouped = work.tile([P, P, 4], BF16, align_bytes=64)
            nc.scalar.copy(out=grouped[:], in_=ht[:].rearrange("p t r -> p r t"))
            h_grouped.append(grouped)
        for g in halves:
            tokens = slice(P * g, P * (g + 1))
            nc.vector.quantize_mx(
                out=h_codes[:, tokens].bitcast(FP8X4),
                scales=h_scales[:, tokens],
                in_=h_grouped[g][:].rearrange("p r t -> p (r t)"),
            )

        n0 = 0
        for i, width in enumerate(STORES):
            result = results.tile([P, width], F32, name="result%d" % i)
            for h in range(width // N_TILE):
                start = n0 % DOWN_COLS
                acc_out = psum_acc.tile([P, N_TILE], F32, tag="acc")
                for g in range(PASSES_2):
                    tokens = slice(P * g, P * (g + 1))
                    nc.tensor.matmul_mx(
                        out=acc_out[:],
                        lhsT=h_codes[:, tokens].bitcast(FP8X4),
                        lhsT_scale=h_scales[:, tokens],
                        rhs=down_words[n0 // DOWN_COLS][:, g, start : start + N_TILE].bitcast(FP8X4),
                        rhs_scale=down_planes[
                            4 * (n0 // PLANE_COLS) : P, g, n0 % PLANE_COLS : n0 % PLANE_COLS + N_TILE
                        ],
                        start=(g == 0),
                        stop=(g == PASSES_2 - 1),
                    )
                nc.vector.tensor_tensor(
                    out=result[:, N_TILE * h : N_TILE * (h + 1)],
                    in0=acc_out[:],
                    in1=s_bcast[:, DOWN_ROW + n0 // N_TILE, :],
                    op=MULT,
                )
                n0 += N_TILE
            nc.sync.dma_start(out=out_rows[:, n0 - width : n0], in_=result[:])
